import numpy as np
import ml_dtypes


def mxq(x, axis, fmt="e4m3"):
    dtype, down = {"e4m3": (ml_dtypes.float8_e4m3fn, 7), "e5m2": (ml_dtypes.float8_e5m2, 14)}[fmt]
    v = np.moveaxis(np.asarray(x, np.float32).astype(ml_dtypes.bfloat16).astype(np.float64), axis, -1)
    blocks = v.reshape(v.shape[:-1] + (-1, 32))
    amax = np.abs(blocks).max(-1, keepdims=True)
    byte = np.maximum(np.where(amax > 0, np.frexp(amax)[1] - 1 + 127, 0) - down, 1)
    scale = np.exp2(byte - 127.0)
    codes = (blocks / scale).astype(np.float32).astype(dtype).astype(np.float64)
    return np.moveaxis((codes * scale).reshape(v.shape), -1, axis)


WIDE = False


def mx_kscale(k):
    if not WIDE:
        return np.ones(k)
    levels = np.array([18, -18])
    if k % 512:
        return np.exp2(np.random.permutation(np.resize(levels, k // 32))).repeat(32)
    a = np.empty((k // 512, 16))
    for p in range(k // 512):
        a[p, :8] = np.random.permutation(np.resize(levels, 8))
        for g in range(8):
            far = levels[np.abs(levels - a[p, g]) >= 10]
            a[p, g + 8] = far[np.random.randint(len(far))]
    return np.exp2(a.ravel()).repeat(32)


BF16 = ml_dtypes.bfloat16


def bf(x):
    return np.asarray(x, np.float32).astype(BF16)


def f64(x):
    return np.asarray(x).astype(np.float64)


B, IN, MEM = 512, 1024, 1024


def sigmoid(v):
    return 1.0 / (1.0 + np.exp(-v))


def setup_inputs():
    s = mx_kscale(B)[:, None]
    u = mx_kscale(MEM)
    w0 = bf(np.random.standard_normal((MEM, MEM + IN)) / np.sqrt(MEM + IN))
    x0 = bf(np.random.standard_normal((B, IN)))
    m0 = bf(np.random.standard_normal((B, MEM)))
    b = bf(np.random.standard_normal(MEM) * 0.3)
    z = np.concatenate([f64(m0), f64(x0)], axis=-1) @ f64(w0).T + f64(b)
    g = bf(8.0 * np.random.standard_normal((B, MEM)) * np.exp2(np.random.randint(-6, 1, (B, 1))) / (s * s) * u)
    return {"input_tensor": bf(f64(x0) * s),
            "previous_memory": bf(f64(m0) * s),
            "fg_w": bf(f64(w0) / u[:, None]),
            "fg_b": b,
            "z": np.asarray(z, np.float32),
            "grad_out": g}


def reference(input_tensor, previous_memory, fg_w, fg_b, z, grad_out):
    m = f64(previous_memory)
    fgate = sigmoid(f64(z))
    dz = f64(grad_out) * m * (fgate * (1.0 - fgate))
    forget_in = np.concatenate([m, f64(input_tensor)], axis=-1)
    w_in = f64(fg_w)[:, MEM:]
    dx = mxq(dz, 1, "e5m2") @ mxq(w_in, 0, "e4m3")
    dw = mxq(dz, 0, "e5m2").T @ mxq(forget_in, 0, "e4m3")
    return dx, dw

@@ -1,0 +1,237 @@
+from contextlib import ExitStack
+
+import concourse.mybir as mybir
+from concourse.masks import make_identity
+
+TOKENS, FEATS, COLS = 512, 1024, 1024
+FLOPS = 2 * TOKENS * FEATS * COLS + 2 * FEATS * TOKENS * 2 * COLS
+BYTES = 2 * TOKENS * FEATS * 3 + 4 * TOKENS * FEATS + 2 * FEATS * COLS + 4 * TOKENS * COLS + 4 * FEATS * 2 * COLS
+
+F32 = mybir.dt.float32
+BF16 = mybir.dt.bfloat16
+U32 = mybir.dt.uint32
+U8 = mybir.dt.uint8
+E4M3 = mybir.dt.float8_e4m3fn_x4
+E5M2 = mybir.dt.float8_e5m2_x4
+ACT = mybir.ActivationFunctionType
+ALU = mybir.AluOpType
+
+P = 128
+PACK = 4
+W = 512
+
+
+def tile_dynamicmemorycell_pa_v_kernel(
+    tc, input_tensor, previous_memory, fg_w, fg_b, z, grad_out, out_0, out_1
+):
+    nc = tc.nc
+
+    with ExitStack() as ctx:
+        keep = ctx.enter_context(tc.tile_pool(name="keep", bufs=1))
+        results = ctx.enter_context(tc.tile_pool(name="results", bufs=12))
+        acc_pool = ctx.enter_context(tc.psum_pool(name="acc", bufs=6))
+        turn_pool = ctx.enter_context(tc.psum_pool(name="turn", bufs=2))
+
+        def keep_tile(shape, dtype, name):
+            return keep.tile(shape, dtype, name=name, align_bytes=64)
+
+        ident = keep_tile([P, P], F32, "ident")
+        make_identity(nc, ident[:])
+        ctx.enter_context(tc.manual_schedule())
+
+        z_v = z.rearrange("(p j) w -> p j w", j=PACK)
+        g_v = grad_out.rearrange("(p j) w -> p j w", j=PACK)
+        m_v = previous_memory.rearrange("(p j) w -> p j w", j=PACK)
+        x_v = input_tensor.rearrange("(p j) w -> p j w", j=PACK)
+        o0_v = out_0.rearrange("(p j) n -> p j n", j=PACK)
+
+        raw = {}
+        z_t = {}
+
+        def load(key, view, shape):
+            t = keep_tile(shape, BF16, "raw_" + key)
+            nc.sync.dma_start(out=t[:], in_=view)
+            raw[key] = t
+
+        for c in range(2):
+            cols = slice(c * W, (c + 1) * W)
+            load("g%d" % c, g_v[:, :, cols], [P, PACK, W])
+            load("m%d" % c, m_v[:, :, cols], [P, PACK, W])
+            for jj in range(2):
+                t = keep_tile([P, 2, W], F32, "z%d%d" % (c, jj))
+                nc.sync.dma_start(out=t[:], in_=z_v[:, 2 * jj : 2 * jj + 2, cols])
+                z_t[c, jj] = t
+        load("x", x_v, [P, PACK, 2 * W])
+        for g in range(2):
+            rows = fg_w[g * W : (g + 1) * W, FEATS : FEATS + COLS]
+            load("w%d" % g, rows.rearrange("(p t) n -> p t n", t=PACK), [P, PACK, 2 * W])
+
+        warm = keep_tile([P, 8], F32, "warm")
+        nc.vector.memset(warm[:], 0.0)
+        nc.scalar.activation(out=warm[:, 0:1], in_=warm[:, 4:5], func=ACT.Tanh)
+
+        sq_t, gm_t, dz_t = {}, {}, {}
+        for c in range(2):
+            t = keep_tile([P, PACK, W], BF16, "dz%d" % c)
+            dz_t[c] = t
+            for jj in range(2):
+                s = keep_tile([P, 2 * W], F32, "sq%d%d" % (c, jj))
+                sq_t[c, jj] = s
+                u = keep_tile([P, 2 * W], F32, "gm%d%d" % (c, jj))
+                gm_t[c, jj] = u
+
+        def square_tanh(c, jj):
+            zf = z_t[c, jj][:].rearrange("p j w -> p (j w)")
+            nc.scalar.activation(out=sq_t[c, jj][:], in_=zf, func=ACT.Tanh, scale=0.5)
+            nc.scalar.activation(out=sq_t[c, jj][:], in_=sq_t[c, jj][:], func=ACT.Square)
+
+        def grad_memory(c, jj):
+            part = slice(2 * jj * W, (2 * jj + 2) * W)
+            nc.vector.scalar_tensor_tensor(
+                out=gm_t[c, jj][:],
+                in0=raw["g%d" % c][:].rearrange("p j w -> p (j w)")[:, part],
+                scalar=-0.25,
+                in1=raw["m%d" % c][:].rearrange("p j w -> p (j w)")[:, part],
+                op0=ALU.mult,
+                op1=ALU.mult,
+            )
+
+        def finish_dz(c, jj):
+            part = slice(2 * jj * W, (2 * jj + 2) * W)
+            nc.vector.scalar_tensor_tensor(
+                out=dz_t[c][:].rearrange("p j w -> p (j w)")[:, part],
+                in0=sq_t[c, jj][:],
+                scalar=1.0,
+                in1=gm_t[c, jj][:],
+                op0=ALU.subtract,
+                op1=ALU.mult,
+            )
+
+        source = {}
+        for c in range(2):
+            cols = slice(c * W, (c + 1) * W)
+            source["d%d" % c] = dz_t[c][:]
+            source["m%d" % c] = raw["m%d" % c][:]
+            source["x%d" % c] = raw["x"][:, :, cols]
+            for g in range(2):
+                source["w%d%d" % (g, c)] = raw["w%d" % g][:, :, cols]
+        grouped, codes, scales = {}, {}, {}
+        for key in ("d0", "d1", "m0", "m1", "x0", "x1", "w00", "w01", "w10", "w11", "f0", "f1"):
+            a = keep_tile([P, W, PACK], BF16, "grouped_" + key)
+            b = keep_tile([P, W], U32, "codes_" + key)
+            s = keep_tile([P, W], U8, "scales_" + key)
+            grouped[key], codes[key], scales[key] = a, b, s
+        fmt = {key: E5M2 if key[0] in "df" else E4M3 for key in grouped}
+
+        def interleave(copy, key, lo, hi):
+            dst = grouped[key][:, lo:hi, :].rearrange("p (c i) t -> p c t i", i=4)
+            src = source[key][:, :, lo:hi].rearrange("p t (c i) -> p c t i", i=4)
+            copy(out=dst, in_=src)
+
+        def quantize(key):
+            nc.vector.quantize_mx(
+                out=codes[key][:].bitcast(fmt[key]),
+                scales=scales[key][:],
+                in_=grouped[key][:].rearrange("p w j -> p (w j)"),
+            )
+
+        def multiply(acc, left, block, right, start, stop):
+            cols = slice(block * P, (block + 1) * P)
+            nc.tensor.matmul_mx(
+                out=acc[:],
+                lhsT=codes[left][:, cols].bitcast(fmt[left]),
+                lhsT_scale=scales[left][:, cols],
+                rhs=codes[right][:].bitcast(fmt[right]),
+                rhs_scale=scales[right][:],
+                start=start,
+                stop=stop,
+            )
+
+        turned = {}
+
+        def transpose(c, jp):
+            words = dz_t[c][:].rearrange("p j w -> p (j w)").bitcast(F32)
+            bank = turn_pool.tile([P, 2, 2, P], F32, name="bank")
+            for jl in range(2):
+                base = (2 * jp + jl) * (W // 2)
+                for u in range(2):
+                    nc.tensor.transpose(bank[:, jl, u, :], words[:, base + u : base + W // 2 : 2], ident[:])
+            turned[c, jp] = bank
+
+        def empty_transpose(copy, c, jp):
+            dst = grouped["f%d" % c][:].rearrange("p n t -> p (n t)").bitcast(F32)
+            dst = dst.rearrange("p (j r u) -> p j r u", j=PACK, u=2)[:, 2 * jp : 2 * jp + 2]
+            copy(out=dst, in_=turned[c, jp][:].rearrange("p j u r -> p j r u"))
+
+        vec, act = nc.vector.tensor_copy, nc.scalar.copy
+
+        def weight_rows(c, f, src, copies):
+            res = results.tile([P, 2 * W], F32, name="res")
+            for h in range(2):
+                acc = acc_pool.tile([P, W], F32, name="accum")
+                multiply(acc, "d%d" % c, f, "%s%d" % (src, h), True, True)
+                copies[h](out=res[:, h * W : (h + 1) * W], in_=acc[:])
+            first = (c * 4 + f) * P
+            col0 = 0 if src == "m" else COLS
+            nc.sync.dma_start(out=out_1[first : first + P, col0 : col0 + COLS], in_=res[:])
+
+        def input_rows(j, copies):
+            res = results.tile([P, 2 * W], F32, name="res")
+            for h in range(2):
+                acc = acc_pool.tile([P, W], F32, name="accum")
+                for g in range(2):
+                    multiply(acc, "f%d" % g, j, "w%d%d" % (g, h), g == 0, g == 1)
+                copies[h](out=res[:, h * W : (h + 1) * W], in_=acc[:])
+            nc.sync.dma_start(out=o0_v[:, j, :], in_=res[:])
+
+        grad_memory(0, 0)
+        interleave(act, "m0", 0, 256)
+        grad_memory(0, 1)
+        interleave(vec, "m0", 256, 512)
+        square_tanh(0, 0)
+        square_tanh(0, 1)
+        finish_dz(0, 0)
+        quantize("m0")
+        grad_memory(1, 0)
+        finish_dz(0, 1)
+        interleave(vec, "m1", 0, 512)
+        interleave(vec, "d0", 0, 512)
+        quantize("m1")
+        square_tanh(1, 0)
+        grad_memory(1, 1)
+        quantize("d0")
+        square_tanh(1, 1)
+        for f in range(4):
+            weight_rows(0, f, "m", (act, act))
+        finish_dz(1, 0)
+        interleave(vec, "x0", 0, 256)
+        finish_dz(1, 1)
+        interleave(vec, "x0", 256, 512)
+        interleave(vec, "d1", 0, 512)
+        quantize("x0")
+        interleave(vec, "x1", 0, 256)
+        quantize("d1")
+        for c in range(2):
+            for jp in range(2):
+                transpose(c, jp)
+                empty_transpose(act, c, jp)
+        for f in range(4):
+            weight_rows(1, f, "m", (act, act))
+        interleave(vec, "x1", 256, 512)
+        interleave(vec, "w00", 0, 512)
+        quantize("x1")
+        for f in range(4):
+            weight_rows(0, f, "x", (act, act))
+        quantize("f0")
+        interleave(vec, "w10", 0, 512)
+        quantize("w00")
+        interleave(vec, "w01", 0, 512)
+        quantize("w10")
+        interleave(vec, "w11", 0, 512)
+        quantize("w01")
+        quantize("f1")
+        quantize("w11")
+        for f in range(4):
+            weight_rows(1, f, "x", (act, vec))
+        for j in range(4):
+            input_rows(j, (act, vec))

@@ -28,9 +28,8 @@ def tile_dynamicmemorycell_pa_v_kernel(
 
     with ExitStack() as ctx:
         keep = ctx.enter_context(tc.tile_pool(name="keep", bufs=1))
-        results = ctx.enter_context(tc.tile_pool(name="results", bufs=12))
-        acc_pool = ctx.enter_context(tc.psum_pool(name="acc", bufs=6))
-        turn_pool = ctx.enter_context(tc.psum_pool(name="turn", bufs=2))
+        results = ctx.enter_context(tc.tile_pool(name="results", bufs=8))
+        acc_pool = ctx.enter_context(tc.psum_pool(name="acc", bufs=8))
 
         def keep_tile(shape, dtype, name):
             return keep.tile(shape, dtype, name=name, align_bytes=64)
@@ -48,23 +47,31 @@ def tile_dynamicmemorycell_pa_v_kernel(
         raw = {}
         z_t = {}
 
-        def load(key, view, shape):
-            t = keep_tile(shape, BF16, "raw_" + key)
-            nc.sync.dma_start(out=t[:], in_=view)
+        def raw_tile(key, cols, dtype):
+            t = keep_tile([P, PACK, cols], dtype, "raw_" + key)
             raw[key] = t
 
+        def load(key, view, lo, hi):
+            nc.sync.dma_start(out=raw[key][:, lo:hi, :], in_=view[:, lo:hi, :])
+
         for c in range(2):
-            cols = slice(c * W, (c + 1) * W)
-            load("g%d" % c, g_v[:, :, cols], [P, PACK, W])
-            load("m%d" % c, m_v[:, :, cols], [P, PACK, W])
-            for jj in range(2):
-                t = keep_tile([P, 2, W], F32, "z%d%d" % (c, jj))
-                nc.sync.dma_start(out=t[:], in_=z_v[:, 2 * jj : 2 * jj + 2, cols])
-                z_t[c, jj] = t
-        load("x", x_v, [P, PACK, 2 * W])
+            raw_tile("z%d" % c, W, F32)
+            raw_tile("g%d" % c, W, BF16)
+            raw_tile("m%d" % c, W, BF16)
+        raw_tile("x", 2 * W, BF16)
+        for g in range(2):
+            raw_tile("w%d" % g, 2 * W, BF16)
+        lo_cols, hi_cols = slice(0, W), slice(W, 2 * W)
+        for key, lo, hi in (("z", 0, 1), ("g", 0, 2), ("m", 0, 2), ("z", 1, 2), ("z", 2, 4), ("g", 2, 4), ("m", 2, 4)):
+            view = {"z": z_v, "g": g_v, "m": m_v}[key]
+            load(key + "0", view[:, :, lo_cols], lo, hi)
+        for key, lo, hi in (("z", 0, 2), ("g", 0, 4), ("m", 0, 4), ("z", 2, 4)):
+            view = {"z": z_v, "g": g_v, "m": m_v}[key]
+            load(key + "1", view[:, :, hi_cols], lo, hi)
+        load("x", x_v, 0, PACK)
         for g in range(2):
             rows = fg_w[g * W : (g + 1) * W, FEATS : FEATS + COLS]
-            load("w%d" % g, rows.rearrange("(p t) n -> p t n", t=PACK), [P, PACK, 2 * W])
+            load("w%d" % g, rows.rearrange("(p t) n -> p t n", t=PACK), 0, PACK)
 
         warm = keep_tile([P, 8], F32, "warm")
         nc.vector.memset(warm[:], 0.0)
@@ -72,54 +79,49 @@ def tile_dynamicmemorycell_pa_v_kernel(
 
         sq_t, gm_t, dz_t = {}, {}, {}
         for c in range(2):
-            t = keep_tile([P, PACK, W], BF16, "dz%d" % c)
-            dz_t[c] = t
-            for jj in range(2):
-                s = keep_tile([P, 2 * W], F32, "sq%d%d" % (c, jj))
-                sq_t[c, jj] = s
-                u = keep_tile([P, 2 * W], F32, "gm%d%d" % (c, jj))
-                gm_t[c, jj] = u
+            d = keep_tile([P, PACK, W], BF16, "dz%d" % c)
+            u = keep_tile([P, PACK, W], F32, "gm%d" % c)
+            dz_t[c], sq_t[c], gm_t[c] = d, raw["z%d" % c], u
 
-        def square_tanh(c, jj):
-            zf = z_t[c, jj][:].rearrange("p j w -> p (j w)")
-            nc.scalar.activation(out=sq_t[c, jj][:], in_=zf, func=ACT.Tanh, scale=0.5)
-            nc.scalar.activation(out=sq_t[c, jj][:], in_=sq_t[c, jj][:], func=ACT.Square)
+        def flat(tile, lo, hi):
+            return tile[:, lo:hi, :].rearrange("p j w -> p (j w)")
 
-        def grad_memory(c, jj):
-            part = slice(2 * jj * W, (2 * jj + 2) * W)
+        def tanh(c, lo, hi):
+            nc.scalar.activation(out=flat(sq_t[c], lo, hi), in_=flat(raw["z%d" % c], lo, hi), func=ACT.Tanh, scale=0.5)
+
+        def square(c, lo, hi):
+            nc.scalar.activation(out=flat(sq_t[c], lo, hi), in_=flat(sq_t[c], lo, hi), func=ACT.Square)
+
+        def grad_memory(c, lo, hi):
             nc.vector.scalar_tensor_tensor(
-                out=gm_t[c, jj][:],
-                in0=raw["g%d" % c][:].rearrange("p j w -> p (j w)")[:, part],
+                out=flat(gm_t[c], lo, hi),
+                in0=flat(raw["g%d" % c], lo, hi),
                 scalar=-0.25,
-                in1=raw["m%d" % c][:].rearrange("p j w -> p (j w)")[:, part],
+                in1=flat(raw["m%d" % c], lo, hi),
                 op0=ALU.mult,
                 op1=ALU.mult,
             )
 
-        def finish_dz(c, jj):
-            part = slice(2 * jj * W, (2 * jj + 2) * W)
+        def finish_dz(c, lo, hi):
             nc.vector.scalar_tensor_tensor(
-                out=dz_t[c][:].rearrange("p j w -> p (j w)")[:, part],
-                in0=sq_t[c, jj][:],
+                out=flat(dz_t[c], lo, hi),
+                in0=flat(sq_t[c], lo, hi),
                 scalar=1.0,
-                in1=gm_t[c, jj][:],
+                in1=flat(gm_t[c], lo, hi),
                 op0=ALU.subtract,
                 op1=ALU.mult,
             )
 
-        source = {}
+        source = {"x": raw["x"], "w0": raw["w0"], "w1": raw["w1"]}
         for c in range(2):
-            cols = slice(c * W, (c + 1) * W)
-            source["d%d" % c] = dz_t[c][:]
-            source["m%d" % c] = raw["m%d" % c][:]
-            source["x%d" % c] = raw["x"][:, :, cols]
-            for g in range(2):
-                source["w%d%d" % (g, c)] = raw["w%d" % g][:, :, cols]
+            source["d%d" % c] = dz_t[c]
+            source["m%d" % c] = raw["m%d" % c]
         grouped, codes, scales = {}, {}, {}
-        for key in ("d0", "d1", "m0", "m1", "x0", "x1", "w00", "w01", "w10", "w11", "f0", "f1"):
-            a = keep_tile([P, W, PACK], BF16, "grouped_" + key)
-            b = keep_tile([P, W], U32, "codes_" + key)
-            s = keep_tile([P, W], U8, "scales_" + key)
+        for key in ("d0", "d1", "m0", "m1", "x", "w0", "w1", "f0", "f1"):
+            width = 2 * W if key[0] in "xw" else W
+            a = keep_tile([P, width, PACK], BF16, "grouped_" + key)
+            b = keep_tile([P, width], U32, "codes_" + key)
+            s = keep_tile([P, width], U8, "scales_" + key)
             grouped[key], codes[key], scales[key] = a, b, s
         fmt = {key: E5M2 if key[0] in "df" else E4M3 for key in grouped}
 
@@ -128,21 +130,22 @@ def tile_dynamicmemorycell_pa_v_kernel(
             src = source[key][:, :, lo:hi].rearrange("p t (c i) -> p c t i", i=4)
             copy(out=dst, in_=src)
 
-        def quantize(key):
+        def quantize(key, lo, hi):
             nc.vector.quantize_mx(
-                out=codes[key][:].bitcast(fmt[key]),
-                scales=scales[key][:],
-                in_=grouped[key][:].rearrange("p w j -> p (w j)"),
+                out=codes[key][:, lo:hi].bitcast(fmt[key]),
+                scales=scales[key][:, lo:hi],
+                in_=grouped[key][:, lo:hi, :].rearrange("p w j -> p (w j)"),
             )
 
-        def multiply(acc, left, block, right, start, stop):
+        def multiply(acc, left, block, right, half, start, stop):
             cols = slice(block * P, (block + 1) * P)
+            wide = slice(half * W, (half + 1) * W)
             nc.tensor.matmul_mx(
                 out=acc[:],
                 lhsT=codes[left][:, cols].bitcast(fmt[left]),
                 lhsT_scale=scales[left][:, cols],
-                rhs=codes[right][:].bitcast(fmt[right]),
-                rhs_scale=scales[right][:],
+                rhs=codes[right][:, wide].bitcast(fmt[right]),
+                rhs_scale=scales[right][:, wide],
                 start=start,
                 stop=stop,
             )
@@ -151,7 +154,7 @@ def tile_dynamicmemorycell_pa_v_kernel(
 
         def transpose(c, jp):
             words = dz_t[c][:].rearrange("p j w -> p (j w)").bitcast(F32)
-            bank = turn_pool.tile([P, 2, 2, P], F32, name="bank")
+            bank = acc_pool.tile([P, 2, 2, P], F32, name="bank")
             for jl in range(2):
                 base = (2 * jp + jl) * (W // 2)
                 for u in range(2):
@@ -159,79 +162,117 @@ def tile_dynamicmemorycell_pa_v_kernel(
             turned[c, jp] = bank
 
         def empty_transpose(copy, c, jp):
-            dst = grouped["f%d" % c][:].rearrange("p n t -> p (n t)").bitcast(F32)
-            dst = dst.rearrange("p (j r u) -> p j r u", j=PACK, u=2)[:, 2 * jp : 2 * jp + 2]
+            dst = grouped["f%d" % c][:, jp * (W // 2) : (jp + 1) * (W // 2), :].rearrange("p n t -> p (n t)").bitcast(F32)
+            dst = dst.rearrange("p (j r u) -> p j r u", j=2, u=2)
             copy(out=dst, in_=turned[c, jp][:].rearrange("p j u r -> p j r u"))
 
         vec, act = nc.vector.tensor_copy, nc.scalar.copy
 
-        def weight_rows(c, f, src, copies):
-            res = results.tile([P, 2 * W], F32, name="res")
-            for h in range(2):
-                acc = acc_pool.tile([P, W], F32, name="accum")
-                multiply(acc, "d%d" % c, f, "%s%d" % (src, h), True, True)
-                copies[h](out=res[:, h * W : (h + 1) * W], in_=acc[:])
-            first = (c * 4 + f) * P
-            col0 = 0 if src == "m" else COLS
-            nc.sync.dma_start(out=out_1[first : first + P, col0 : col0 + COLS], in_=res[:])
+        open_rows = {}
 
-        def input_rows(j, copies):
-            res = results.tile([P, 2 * W], F32, name="res")
-            for h in range(2):
-                acc = acc_pool.tile([P, W], F32, name="accum")
-                for g in range(2):
-                    multiply(acc, "f%d" % g, j, "w%d%d" % (g, h), g == 0, g == 1)
-                copies[h](out=res[:, h * W : (h + 1) * W], in_=acc[:])
-            nc.sync.dma_start(out=o0_v[:, j, :], in_=res[:])
+        def weight_bank(c, f, right, half, copy, part, store):
+            place, banks = part
+            if place == 0:
+                res = results.tile([P, 4 * W], F32, name="res")
+                open_rows[c, f] = res
+            res = open_rows[c, f]
+            acc = acc_pool.tile([P, W], F32, name="bank")
+            multiply(acc, "d%d" % c, f, right, half, True, True)
+            copy(out=res[:, place * W : (place + 1) * W], in_=acc[:])
+            if store is not None:
+                first = (c * 4 + f) * P
+                nc.sync.dma_start(out=out_1[first : first + P, store : store + banks * W], in_=res[:, : banks * W])
 
-        grad_memory(0, 0)
+        def weight_rows(c, f, srcs, copies):
+            col0 = 0 if srcs[0] == M0 else COLS
+            for i, (right, half) in enumerate(srcs):
+                last = i == len(srcs) - 1
+                weight_bank(c, f, right, half, copies[i], (i, len(srcs)), col0 if last else None)
+
+        out_banks = {}
+
+        def open_input(j, h):
+            acc = acc_pool.tile([P, W], F32, name="bank")
+            out_banks[j, h] = acc
+            multiply(acc, "f0", j, "w0", h, True, False)
+
+        def close_input(j, copies):
+            res = results.tile([P, 4 * W], F32, name="res")
+            for h in range(2):
+                acc = out_banks[j, h]
+                multiply(acc, "f1", j, "w1", h, False, True)
+                copies[h](out=res[:, h * W : (h + 1) * W], in_=acc[:])
+            nc.sync.dma_start(out=o0_v[:, j, :], in_=res[:, : 2 * W])
+
+        M0, M1, X0, X1 = ("m0", 0), ("m1", 0), ("x", 0), ("x", 1)
+
+        tanh(0, 0, 1)
+        grad_memory(0, 0, 2)
+        tanh(0, 1, 2)
+        square(0, 0, 2)
+        tanh(0, 2, 4)
+        finish_dz(0, 0, 2)
         interleave(act, "m0", 0, 256)
-        grad_memory(0, 1)
+        grad_memory(0, 2, 4)
+        square(0, 2, 4)
         interleave(vec, "m0", 256, 512)
-        square_tanh(0, 0)
-        square_tanh(0, 1)
-        finish_dz(0, 0)
-        quantize("m0")
-        grad_memory(1, 0)
-        finish_dz(0, 1)
-        interleave(vec, "m1", 0, 512)
+        tanh(1, 0, 2)
+        finish_dz(0, 2, 4)
+        quantize("m0", 0, 512)
         interleave(vec, "d0", 0, 512)
-        quantize("m1")
-        square_tanh(1, 0)
-        grad_memory(1, 1)
-        quantize("d0")
-        square_tanh(1, 1)
+        interleave(act, "m1", 0, 256)
+        interleave(vec, "m1", 256, 512)
+        quantize("d0", 0, 512)
+        square(1, 0, 2)
+        quantize("m1", 0, 512)
+        tanh(1, 2, 4)
         for f in range(4):
-            weight_rows(0, f, "m", (act, act))
-        finish_dz(1, 0)
-        interleave(vec, "x0", 0, 256)
-        finish_dz(1, 1)
-        interleave(vec, "x0", 256, 512)
+            weight_bank(0, f, "m0", 0, act, (0, 2), None)
+        interleave(vec, "x", 0, 512)
+        grad_memory(1, 0, 2)
+        for f in range(4):
+            weight_bank(0, f, "m1", 0, act, (1, 2), 0)
+        quantize("x", 0, 512)
+        square(1, 2, 4)
+        interleave(vec, "x", 512, 1024)
+        grad_memory(1, 2, 4)
+        quantize("x", 512, 1024)
+        finish_dz(1, 0, 2)
+        for jp in range(2):
+            transpose(0, jp)
+            empty_transpose(act, 0, jp)
+        for f in range(4):
+            weight_rows(0, f, (X0, X1), (act, act))
+        finish_dz(1, 2, 4)
+        quantize("f0", 0, 512)
         interleave(vec, "d1", 0, 512)
-        quantize("x0")
-        interleave(vec, "x1", 0, 256)
-        quantize("d1")
-        for c in range(2):
-            for jp in range(2):
-                transpose(c, jp)
-                empty_transpose(act, c, jp)
-        for f in range(4):
-            weight_rows(1, f, "m", (act, act))
-        interleave(vec, "x1", 256, 512)
-        interleave(vec, "w00", 0, 512)
-        quantize("x1")
-        for f in range(4):
-            weight_rows(0, f, "x", (act, act))
-        quantize("f0")
-        interleave(vec, "w10", 0, 512)
-        quantize("w00")
-        interleave(vec, "w01", 0, 512)
-        quantize("w10")
-        interleave(vec, "w11", 0, 512)
-        quantize("w01")
-        quantize("f1")
-        quantize("w11")
-        for f in range(4):
-            weight_rows(1, f, "x", (act, vec))
-        for j in range(4):
-            input_rows(j, (act, vec))
+        interleave(vec, "w0", 0, 512)
+        quantize("d1", 0, 512)
+        interleave(vec, "w0", 512, 1024)
+        for jp in range(2):
+            transpose(1, jp)
+            empty_transpose(act, 1, jp)
+        interleave(vec, "w1", 0, 512)
+        quantize("w0", 0, 1024)
+        for f in range(2):
+            weight_rows(1, f, (M0, M1), (act, act))
+            weight_rows(1, f, (X0, X1), (act, act))
+        interleave(vec, "w1", 512, 1024)
+        quantize("f1", 0, 512)
+        open_input(0, 0)
+        open_input(0, 1)
+        quantize("w1", 0, 1024)
+        weight_rows(1, 2, (M0, M1), (act, act))
+        weight_rows(1, 2, (X0, X1), (act, act))
+        open_input(1, 0)
+        open_input(1, 1)
+        close_input(0, (act, vec))
+        weight_rows(1, 3, (M0, M1), (act, vec))
+        close_input(1, (act, vec))
+        open_input(2, 0)
+        open_input(2, 1)
+        weight_rows(1, 3, (X0, X1), (act, vec))
+        open_input(3, 0)
+        open_input(3, 1)
+        close_input(2, (act, vec))
+        close_input(3, (act, vec))

@@ -62,10 +62,10 @@ def tile_dynamicmemorycell_pa_v_kernel(
         for g in range(2):
             raw_tile("w%d" % g, 2 * W, BF16)
         lo_cols, hi_cols = slice(0, W), slice(W, 2 * W)
-        for key, lo, hi in (("z", 0, 1), ("g", 0, 2), ("m", 0, 2), ("z", 1, 2), ("z", 2, 4), ("g", 2, 4), ("m", 2, 4)):
+        for key, lo, hi in (("z", 0, 2), ("g", 0, 2), ("m", 0, 2), ("g", 2, 4), ("m", 2, 4), ("z", 2, 4)):
             view = {"z": z_v, "g": g_v, "m": m_v}[key]
             load(key + "0", view[:, :, lo_cols], lo, hi)
-        for key, lo, hi in (("z", 0, 2), ("g", 0, 4), ("m", 0, 4), ("z", 2, 4)):
+        for key, lo, hi in (("z", 0, 2), ("m", 0, 4), ("g", 0, 4), ("z", 2, 4)):
             view = {"z": z_v, "g": g_v, "m": m_v}[key]
             load(key + "1", view[:, :, hi_cols], lo, hi)
         load("x", x_v, 0, PACK)
@@ -190,57 +190,58 @@ def tile_dynamicmemorycell_pa_v_kernel(
                 weight_bank(c, f, right, half, copies[i], (i, len(srcs)), col0 if last else None)
 
         out_banks = {}
+        out_rows = {}
 
         def open_input(j, h):
             acc = acc_pool.tile([P, W], F32, name="bank")
             out_banks[j, h] = acc
             multiply(acc, "f0", j, "w0", h, True, False)
 
-        def close_input(j, copies):
-            res = results.tile([P, 4 * W], F32, name="res")
-            for h in range(2):
-                acc = out_banks[j, h]
-                multiply(acc, "f1", j, "w1", h, False, True)
-                copies[h](out=res[:, h * W : (h + 1) * W], in_=acc[:])
-            nc.sync.dma_start(out=o0_v[:, j, :], in_=res[:, : 2 * W])
+        def close_input(j, h, copy):
+            acc = out_banks[j, h]
+            multiply(acc, "f1", j, "w1", h, False, True)
+            if h == 0:
+                res = results.tile([P, 4 * W], F32, name="res")
+                out_rows[j] = res
+            res = out_rows[j]
+            copy(out=res[:, h * W : (h + 1) * W], in_=acc[:])
+            if h == 1:
+                nc.sync.dma_start(out=o0_v[:, j, :], in_=res[:, : 2 * W])
 
         M0, M1, X0, X1 = ("m0", 0), ("m1", 0), ("x", 0), ("x", 1)
 
-        tanh(0, 0, 1)
-        grad_memory(0, 0, 2)
-        tanh(0, 1, 2)
+        tanh(0, 0, 2)
         square(0, 0, 2)
-        tanh(0, 2, 4)
+        grad_memory(0, 0, 2)
         finish_dz(0, 0, 2)
         interleave(act, "m0", 0, 256)
+        tanh(0, 2, 4)
         grad_memory(0, 2, 4)
         square(0, 2, 4)
         interleave(vec, "m0", 256, 512)
-        tanh(1, 0, 2)
-        finish_dz(0, 2, 4)
         quantize("m0", 0, 512)
+        finish_dz(0, 2, 4)
+        tanh(1, 0, 2)
+        interleave(vec, "m1", 256, 512)
         interleave(vec, "d0", 0, 512)
         interleave(act, "m1", 0, 256)
-        interleave(vec, "m1", 256, 512)
+        grad_memory(1, 0, 2)
         quantize("d0", 0, 512)
         square(1, 0, 2)
         quantize("m1", 0, 512)
         tanh(1, 2, 4)
-        for f in range(4):
-            weight_bank(0, f, "m0", 0, act, (0, 2), None)
-        interleave(vec, "x", 0, 512)
-        grad_memory(1, 0, 2)
-        for f in range(4):
-            weight_bank(0, f, "m1", 0, act, (1, 2), 0)
-        quantize("x", 0, 512)
         square(1, 2, 4)
-        interleave(vec, "x", 512, 1024)
-        grad_memory(1, 2, 4)
-        quantize("x", 512, 1024)
-        finish_dz(1, 0, 2)
         for jp in range(2):
             transpose(0, jp)
             empty_transpose(act, 0, jp)
+        interleave(vec, "x", 0, 512)
+        for f in range(4):
+            weight_rows(0, f, (M0, M1), (act, act))
+        grad_memory(1, 2, 4)
+        quantize("x", 0, 512)
+        interleave(vec, "x", 512, 1024)
+        finish_dz(1, 0, 2)
+        quantize("x", 512, 1024)
         for f in range(4):
             weight_rows(0, f, (X0, X1), (act, act))
         finish_dz(1, 2, 4)
@@ -259,20 +260,23 @@ def tile_dynamicmemorycell_pa_v_kernel(
             weight_rows(1, f, (X0, X1), (act, act))
         interleave(vec, "w1", 512, 1024)
         quantize("f1", 0, 512)
+        quantize("w1", 0, 1024)
         open_input(0, 0)
         open_input(0, 1)
-        quantize("w1", 0, 1024)
         weight_rows(1, 2, (M0, M1), (act, act))
         weight_rows(1, 2, (X0, X1), (act, act))
         open_input(1, 0)
         open_input(1, 1)
-        close_input(0, (act, vec))
+        close_input(0, 0, act)
+        close_input(0, 1, vec)
         weight_rows(1, 3, (M0, M1), (act, vec))
-        close_input(1, (act, vec))
+        close_input(1, 0, act)
+        close_input(1, 1, vec)
         open_input(2, 0)
         open_input(2, 1)
         weight_rows(1, 3, (X0, X1), (act, vec))
         open_input(3, 0)
         open_input(3, 1)
-        close_input(2, (act, vec))
-        close_input(3, (act, vec))
+        for j in range(2, 4):
+            close_input(j, 0, act)
+            close_input(j, 1, vec)

from contextlib import ExitStack

import concourse.mybir as mybir
from concourse.masks import make_identity

TOKENS, FEATS, COLS = 512, 1024, 1024
FLOPS = 2 * TOKENS * FEATS * COLS + 2 * FEATS * TOKENS * 2 * COLS
BYTES = 2 * TOKENS * FEATS * 3 + 4 * TOKENS * FEATS + 2 * FEATS * COLS + 4 * TOKENS * COLS + 4 * FEATS * 2 * COLS

F32 = mybir.dt.float32
BF16 = mybir.dt.bfloat16
U32 = mybir.dt.uint32
U8 = mybir.dt.uint8
E4M3 = mybir.dt.float8_e4m3fn_x4
E5M2 = mybir.dt.float8_e5m2_x4
ACT = mybir.ActivationFunctionType
ALU = mybir.AluOpType

P = 128
PACK = 4
W = 512


def tile_dynamicmemorycell_pa_v_kernel(
    tc, input_tensor, previous_memory, fg_w, fg_b, z, grad_out, out_0, out_1
):
    nc = tc.nc

    with ExitStack() as ctx:
        keep = ctx.enter_context(tc.tile_pool(name="keep", bufs=1))
        results = ctx.enter_context(tc.tile_pool(name="results", bufs=8))
        acc_pool = ctx.enter_context(tc.psum_pool(name="acc", bufs=8))

        def keep_tile(shape, dtype, name):
            return keep.tile(shape, dtype, name=name, align_bytes=64)

        ident = keep_tile([P, P], F32, "ident")
        make_identity(nc, ident[:])
        ctx.enter_context(tc.manual_schedule())

        z_v = z.rearrange("(p j) w -> p j w", j=PACK)
        g_v = grad_out.rearrange("(p j) w -> p j w", j=PACK)
        m_v = previous_memory.rearrange("(p j) w -> p j w", j=PACK)
        x_v = input_tensor.rearrange("(p j) w -> p j w", j=PACK)
        o0_v = out_0.rearrange("(p j) n -> p j n", j=PACK)

        raw = {}
        z_t = {}

        def raw_tile(key, cols, dtype):
            t = keep_tile([P, PACK, cols], dtype, "raw_" + key)
            raw[key] = t

        def load(key, view, lo, hi):
            nc.sync.dma_start(out=raw[key][:, lo:hi, :], in_=view[:, lo:hi, :])

        for c in range(2):
            raw_tile("z%d" % c, W, F32)
            raw_tile("g%d" % c, W, BF16)
            raw_tile("m%d" % c, W, BF16)
        raw_tile("x", 2 * W, BF16)
        for g in range(2):
            raw_tile("w%d" % g, 2 * W, BF16)
        lo_cols, hi_cols = slice(0, W), slice(W, 2 * W)
        for key, lo, hi in (("z", 0, 2), ("g", 0, 2), ("m", 0, 2), ("g", 2, 4), ("m", 2, 4), ("z", 2, 4)):
            view = {"z": z_v, "g": g_v, "m": m_v}[key]
            load(key + "0", view[:, :, lo_cols], lo, hi)
        for key, lo, hi in (("z", 0, 2), ("m", 0, 4), ("g", 0, 4), ("z", 2, 4)):
            view = {"z": z_v, "g": g_v, "m": m_v}[key]
            load(key + "1", view[:, :, hi_cols], lo, hi)
        load("x", x_v, 0, PACK)
        for g in range(2):
            rows = fg_w[g * W : (g + 1) * W, FEATS : FEATS + COLS]
            load("w%d" % g, rows.rearrange("(p t) n -> p t n", t=PACK), 0, PACK)

        warm = keep_tile([P, 8], F32, "warm")
        nc.vector.memset(warm[:], 0.0)
        nc.scalar.activation(out=warm[:, 0:1], in_=warm[:, 4:5], func=ACT.Tanh)

        sq_t, gm_t, dz_t = {}, {}, {}
        for c in range(2):
            d = keep_tile([P, PACK, W], BF16, "dz%d" % c)
            u = keep_tile([P, PACK, W], F32, "gm%d" % c)
            dz_t[c], sq_t[c], gm_t[c] = d, raw["z%d" % c], u

        def flat(tile, lo, hi):
            return tile[:, lo:hi, :].rearrange("p j w -> p (j w)")

        def tanh(c, lo, hi):
            nc.scalar.activation(out=flat(sq_t[c], lo, hi), in_=flat(raw["z%d" % c], lo, hi), func=ACT.Tanh, scale=0.5)

        def square(c, lo, hi):
            nc.scalar.activation(out=flat(sq_t[c], lo, hi), in_=flat(sq_t[c], lo, hi), func=ACT.Square)

        def grad_memory(c, lo, hi):
            nc.vector.scalar_tensor_tensor(
                out=flat(gm_t[c], lo, hi),
                in0=flat(raw["g%d" % c], lo, hi),
                scalar=-0.25,
                in1=flat(raw["m%d" % c], lo, hi),
                op0=ALU.mult,
                op1=ALU.mult,
            )

        def finish_dz(c, lo, hi):
            nc.vector.scalar_tensor_tensor(
                out=flat(dz_t[c], lo, hi),
                in0=flat(sq_t[c], lo, hi),
                scalar=1.0,
                in1=flat(gm_t[c], lo, hi),
                op0=ALU.subtract,
                op1=ALU.mult,
            )

        source = {"x": raw["x"], "w0": raw["w0"], "w1": raw["w1"]}
        for c in range(2):
            source["d%d" % c] = dz_t[c]
            source["m%d" % c] = raw["m%d" % c]
        grouped, codes, scales = {}, {}, {}
        for key in ("d0", "d1", "m0", "m1", "x", "w0", "w1", "f0", "f1"):
            width = 2 * W if key[0] in "xw" else W
            a = keep_tile([P, width, PACK], BF16, "grouped_" + key)
            b = keep_tile([P, width], U32, "codes_" + key)
            s = keep_tile([P, width], U8, "scales_" + key)
            grouped[key], codes[key], scales[key] = a, b, s
        fmt = {key: E5M2 if key[0] in "df" else E4M3 for key in grouped}

        def interleave(copy, key, lo, hi):
            dst = grouped[key][:, lo:hi, :].rearrange("p (c i) t -> p c t i", i=4)
            src = source[key][:, :, lo:hi].rearrange("p t (c i) -> p c t i", i=4)
            copy(out=dst, in_=src)

        def quantize(key, lo, hi):
            nc.vector.quantize_mx(
                out=codes[key][:, lo:hi].bitcast(fmt[key]),
                scales=scales[key][:, lo:hi],
                in_=grouped[key][:, lo:hi, :].rearrange("p w j -> p (w j)"),
            )

        def multiply(acc, left, block, right, half, start, stop):
            cols = slice(block * P, (block + 1) * P)
            wide = slice(half * W, (half + 1) * W)
            nc.tensor.matmul_mx(
                out=acc[:],
                lhsT=codes[left][:, cols].bitcast(fmt[left]),
                lhsT_scale=scales[left][:, cols],
                rhs=codes[right][:, wide].bitcast(fmt[right]),
                rhs_scale=scales[right][:, wide],
                start=start,
                stop=stop,
            )

        turned = {}

        def transpose(c, jp):
            words = dz_t[c][:].rearrange("p j w -> p (j w)").bitcast(F32)
            bank = acc_pool.tile([P, 2, 2, P], F32, name="bank")
            for jl in range(2):
                base = (2 * jp + jl) * (W // 2)
                for u in range(2):
                    nc.tensor.transpose(bank[:, jl, u, :], words[:, base + u : base + W // 2 : 2], ident[:])
            turned[c, jp] = bank

        def empty_transpose(copy, c, jp):
            dst = grouped["f%d" % c][:, jp * (W // 2) : (jp + 1) * (W // 2), :].rearrange("p n t -> p (n t)").bitcast(F32)
            dst = dst.rearrange("p (j r u) -> p j r u", j=2, u=2)
            copy(out=dst, in_=turned[c, jp][:].rearrange("p j u r -> p j r u"))

        vec, act = nc.vector.tensor_copy, nc.scalar.copy

        open_rows = {}

        def weight_bank(c, f, right, half, copy, part, store):
            place, banks = part
            if place == 0:
                res = results.tile([P, 4 * W], F32, name="res")
                open_rows[c, f] = res
            res = open_rows[c, f]
            acc = acc_pool.tile([P, W], F32, name="bank")
            multiply(acc, "d%d" % c, f, right, half, True, True)
            copy(out=res[:, place * W : (place + 1) * W], in_=acc[:])
            if store is not None:
                first = (c * 4 + f) * P
                nc.sync.dma_start(out=out_1[first : first + P, store : store + banks * W], in_=res[:, : banks * W])

        def weight_rows(c, f, srcs, copies):
            col0 = 0 if srcs[0] == M0 else COLS
            for i, (right, half) in enumerate(srcs):
                last = i == len(srcs) - 1
                weight_bank(c, f, right, half, copies[i], (i, len(srcs)), col0 if last else None)

        out_banks = {}
        out_rows = {}

        def open_input(j, h):
            acc = acc_pool.tile([P, W], F32, name="bank")
            out_banks[j, h] = acc
            multiply(acc, "f0", j, "w0", h, True, False)

        def close_input(j, h, copy):
            acc = out_banks[j, h]
            multiply(acc, "f1", j, "w1", h, False, True)
            if h == 0:
                res = results.tile([P, 4 * W], F32, name="res")
                out_rows[j] = res
            res = out_rows[j]
            copy(out=res[:, h * W : (h + 1) * W], in_=acc[:])
            if h == 1:
                nc.sync.dma_start(out=o0_v[:, j, :], in_=res[:, : 2 * W])

        M0, M1, X0, X1 = ("m0", 0), ("m1", 0), ("x", 0), ("x", 1)

        tanh(0, 0, 2)
        square(0, 0, 2)
        grad_memory(0, 0, 2)
        finish_dz(0, 0, 2)
        interleave(act, "m0", 0, 256)
        tanh(0, 2, 4)
        grad_memory(0, 2, 4)
        square(0, 2, 4)
        interleave(vec, "m0", 256, 512)
        quantize("m0", 0, 512)
        finish_dz(0, 2, 4)
        tanh(1, 0, 2)
        interleave(vec, "m1", 256, 512)
        interleave(vec, "d0", 0, 512)
        interleave(act, "m1", 0, 256)
        grad_memory(1, 0, 2)
        quantize("d0", 0, 512)
        square(1, 0, 2)
        quantize("m1", 0, 512)
        tanh(1, 2, 4)
        square(1, 2, 4)
        for jp in range(2):
            transpose(0, jp)
            empty_transpose(act, 0, jp)
        interleave(vec, "x", 0, 512)
        for f in range(4):
            weight_rows(0, f, (M0, M1), (act, act))
        grad_memory(1, 2, 4)
        quantize("x", 0, 512)
        interleave(vec, "x", 512, 1024)
        finish_dz(1, 0, 2)
        quantize("x", 512, 1024)
        for f in range(4):
            weight_rows(0, f, (X0, X1), (act, act))
        finish_dz(1, 2, 4)
        quantize("f0", 0, 512)
        interleave(vec, "d1", 0, 512)
        interleave(vec, "w0", 0, 512)
        quantize("d1", 0, 512)
        interleave(vec, "w0", 512, 1024)
        for jp in range(2):
            transpose(1, jp)
            empty_transpose(act, 1, jp)
        interleave(vec, "w1", 0, 512)
        quantize("w0", 0, 1024)
        for f in range(2):
            weight_rows(1, f, (M0, M1), (act, act))
            weight_rows(1, f, (X0, X1), (act, act))
        interleave(vec, "w1", 512, 1024)
        quantize("f1", 0, 512)
        quantize("w1", 0, 1024)
        open_input(0, 0)
        open_input(0, 1)
        weight_rows(1, 2, (M0, M1), (act, act))
        weight_rows(1, 2, (X0, X1), (act, act))
        open_input(1, 0)
        open_input(1, 1)
        close_input(0, 0, act)
        close_input(0, 1, vec)
        weight_rows(1, 3, (M0, M1), (act, vec))
        close_input(1, 0, act)
        close_input(1, 1, vec)
        open_input(2, 0)
        open_input(2, 1)
        weight_rows(1, 3, (X0, X1), (act, vec))
        open_input(3, 0)
        open_input(3, 1)
        for j in range(2, 4):
            close_input(j, 0, act)
            close_input(j, 1, vec)
